import numpy as np
import ml_dtypes


def mxq(x, axis, fmt="e4m3"):
    dtype, down = {"e4m3": (ml_dtypes.float8_e4m3fn, 7), "e5m2": (ml_dtypes.float8_e5m2, 14)}[fmt]
    v = np.moveaxis(np.asarray(x, np.float32).astype(ml_dtypes.bfloat16).astype(np.float64), axis, -1)
    blocks = v.reshape(v.shape[:-1] + (-1, 32))
    amax = np.abs(blocks).max(-1, keepdims=True)
    byte = np.maximum(np.where(amax > 0, np.frexp(amax)[1] - 1 + 127, 0) - down, 1)
    scale = np.exp2(byte - 127.0)
    codes = (blocks / scale).astype(np.float32).astype(dtype).astype(np.float64)
    return np.moveaxis((codes * scale).reshape(v.shape), -1, axis)


WIDE = False


def mx_kscale(k):
    if not WIDE:
        return np.ones(k)
    levels = np.array([10, -10, 5, -5, 0])
    if k % 512:
        return np.exp2(np.random.permutation(np.resize(levels, k // 32))).repeat(32)
    a = np.empty((k // 512, 16))
    for p in range(k // 512):
        a[p, :8] = np.random.permutation(np.resize(levels, 8))
        for g in range(8):
            far = levels[np.abs(levels - a[p, g]) >= 10]
            a[p, g + 8] = far[np.random.randint(len(far))]
    return np.exp2(a.ravel()).repeat(32)


BF16 = ml_dtypes.bfloat16


def bf(x):
    return np.asarray(x, np.float32).astype(BF16)


def f64(x):
    return np.asarray(x).astype(np.float64)


T, M, HW, D, DK, H = 2, 512, 768, 1024, 1024, 8
EPS = 1e-6
EXTENT = 27.0


def rope_2d(x, pos):
    nt, n, c = x.shape
    half, quarter = c // 2, c // 4
    theta = 100.0 ** (-2.0 * np.arange(quarter) / half)

    def apply(part, p):
        fr = p[..., None] * theta
        cos, sin = np.cos(fr), np.sin(fr)
        pr = part.reshape(nt, n, quarter, 2)
        x1, x2 = pr[..., 0], pr[..., 1]
        return np.stack([x1 * cos - x2 * sin, x1 * sin + x2 * cos], axis=-1).reshape(nt, n, half)

    return np.concatenate([apply(x[:, :, :half], pos[..., 0]), apply(x[:, :, half:], pos[..., 1])], axis=-1)


def layernorm_nobias(x, gamma):
    mu = x.mean(-1, keepdims=True)
    var = ((x - mu) ** 2).mean(-1, keepdims=True)
    return (x - mu) / np.sqrt(var + EPS) * gamma


def setup_inputs():
    s = mx_kscale(D)
    return {"updated_track_tokens": bf(np.random.standard_normal((T, M, D)) * s),
            "tracks": bf(np.random.uniform(0.0, EXTENT, (T, M, 2))),
            "W_k": bf(np.random.standard_normal((DK, D)) / np.sqrt(D) / s),
            "k_gamma": bf(1.0 + 0.1 * np.random.standard_normal(DK))}


def core(updated_track_tokens, tracks, W_k, k_gamma):
    k = mxq(f64(updated_track_tokens), 2, "e4m3") @ mxq(f64(W_k), 1, "e4m3").T
    k = rope_2d(k, f64(tracks))
    return layernorm_nobias(k, f64(k_gamma))


def e4m3fn_bytes(y):
    return np.clip(np.asarray(y, np.float64), -448.0, 448.0).astype(np.float32).astype(ml_dtypes.float8_e4m3fn).view(np.uint8)


def reference(updated_track_tokens, tracks, W_k, k_gamma):
    out = core(updated_track_tokens, tracks, W_k, k_gamma)
    s = np.max(np.abs(out), axis=-1, keepdims=True) / 448.0
    return out, e4m3fn_bytes(out / s)

@@ -1,0 +1,328 @@
+import math
+from contextlib import ExitStack
+
+import concourse.mybir as mybir
+from concourse.masks import make_identity
+
+FLOPS = 2 * 1024 * 1024 * 1024
+
+F32 = mybir.dt.float32
+BF16 = mybir.dt.bfloat16
+I32 = mybir.dt.int32
+U32 = mybir.dt.uint32
+U8 = mybir.dt.uint8
+FP8X4 = mybir.dt.float8_e4m3fn_x4
+FP8 = mybir.dt.float8_e4m3fn
+ALU = mybir.AluOpType
+ACT = mybir.ActivationFunctionType
+AX = mybir.AxisListType
+
+P = 128
+NT = 8
+K = 1024
+C = 1024
+HALF = 512
+EPS = 1e-6
+TWO_PI = 2.0 * math.pi
+RATIO = 100.0 ** (-1.0 / 256.0)
+LAST = NT - 1
+SCALE_ON_G = (1, 3, 5)
+X_CHUNKS = ((0, 1), (1, 2), (2, 4), (4, 8))
+
+
+def tile_attentionalsplatting_pa_kernel(tc, tokens, tracks, w_k, k_gamma, out_0, out_1):
+    nc = tc.nc
+    x_view = tokens.flatten_outer_dims().rearrange("(p t) k -> p t k", t=NT)
+    pos_view = tracks.flatten_outer_dims().rearrange("(p t) c -> p (t c)", t=NT)
+    w_view = w_k.rearrange("(j q h) k -> j q (h k)", j=4, h=2)
+    g_view = k_gamma.rearrange("(o c) -> o c", o=1)
+    o0_view = out_0.flatten_outer_dims().rearrange("(p t) c -> p t c", t=NT)
+    o1_view = out_1.flatten_outer_dims().rearrange("(p t) c -> p t c", t=NT)
+
+    with ExitStack() as ctx:
+        const = ctx.enter_context(tc.tile_pool(name="const", bufs=1))
+        grp = ctx.enter_context(tc.tile_pool(name="grp", bufs=4))
+        rrp = ctx.enter_context(tc.tile_pool(name="rrp", bufs=NT))
+        trig = ctx.enter_context(tc.tile_pool(name="trig", bufs=4))
+        work = ctx.enter_context(tc.tile_pool(name="work", bufs=3))
+        stat = ctx.enter_context(tc.tile_pool(name="stat", bufs=4))
+        tps = ctx.enter_context(tc.psum_pool(name="tps", bufs=4))
+        accp = ctx.enter_context(tc.psum_pool(name="accp", bufs=2))
+        ctx.enter_context(tc.manual_schedule())
+
+        ident = const.tile([P, P], F32, name="ident")
+        make_identity(nc, ident[:])
+        ones_bf = const.tile([P, P], BF16, name="ones_bf")
+        nc.gpsimd.memset(ones_bf[:], 1.0)
+        neghalf = const.tile([P, 1], F32, name="neghalf")
+        nc.gpsimd.memset(neghalf[:], -0.5)
+        zeros = const.tile([P, 1], F32, name="zeros")
+        nc.vector.memset(zeros[:], 0.0)
+        one1 = const.tile([P, 1], F32, name="one1")
+        nc.vector.memset(one1[:], 1.0)
+        g_row = const.tile([P, C], BF16, name="g_row")
+        nc.vector.memset(g_row[:], 0.0)
+        warm = const.tile([P, 1], F32, name="warm")
+        nc.scalar.activation(out=warm[:], in_=zeros[:], func=ACT.Sin)
+
+        pos_bf = const.tile([P, 2 * NT], BF16, name="pos_bf")
+        nc.sync.dma_start(out=pos_bf[:], in_=pos_view)
+        x_words = {}
+
+        def load_x(a, b):
+            xr = const.tile([P, b - a, K], BF16, name="xr%d" % a)
+            nc.sync.dma_start(out=xr[:], in_=x_view[:, a:b, :])
+            for t in range(a, b):
+                x_words[t] = xr[:, t - a, :].bitcast(F32)
+
+        load_x(*X_CHUNKS[0])
+        w_raw = []
+        for j in range(4):
+            wr = const.tile([P, 2, K], BF16, name="wr%d" % j)
+            nc.sync.dma_start(out=wr[:].rearrange("q h k -> q (h k)"), in_=w_view[j])
+            w_raw.append(wr)
+        for a, b in X_CHUNKS[1:]:
+            load_x(a, b)
+        nc.scalar.dma_start(out=g_row[0:1, :], in_=g_view)
+
+        theta = const.tile([P, 256], F32, name="theta")
+        nc.vector.tensor_scalar(out=theta[:, 0:1], in0=one1[:], scalar1=1.0 / TWO_PI, scalar2=None, op0=ALU.mult)
+        for s in (1, 4, 16, 64):
+            for j in (1, 2, 3):
+                nc.vector.tensor_scalar(
+                    out=theta[:, j * s : (j + 1) * s], in0=theta[:, 0:s], scalar1=RATIO ** (j * s), scalar2=None, op0=ALU.mult
+                )
+        pos_f = const.tile([P, 2 * NT], F32, name="pos_f")
+        nc.vector.tensor_copy(out=pos_f[:], in_=pos_bf[:])
+
+        fracs = {}
+        tables = {}
+
+        def rr(t):
+            n_i = rrp.tile([P, HALF], I32, name="n_i", tag="n_i")
+            f = rrp.tile([P, HALF], F32, name="f", tag="f")
+            for c in (0, 1):
+                nc.vector.tensor_scalar(
+                    out=n_i[:, 256 * c : 256 * (c + 1)], in0=theta[:], scalar1=pos_f[:, 2 * t + c : 2 * t + c + 1],
+                    scalar2=None, op0=ALU.mult,
+                )
+            for c in (0, 1):
+                nc.vector.scalar_tensor_tensor(
+                    out=f[:, 256 * c : 256 * (c + 1)], in0=theta[:], scalar=pos_f[:, 2 * t + c : 2 * t + c + 1],
+                    in1=n_i[:, 256 * c : 256 * (c + 1)], op0=ALU.mult, op1=ALU.subtract,
+                )
+            fracs[t] = f
+
+        def trig_tile(t):
+            f = fracs[t]
+            af = work.tile([P, HALF], F32, name="af", tag="af", bufs=2)
+            sin_t = trig.tile([P, HALF], F32, name="sin_t", tag="sin_t")
+            cos_t = trig.tile([P, HALF], F32, name="cos_t", tag="cos_t")
+            nc.scalar.activation(out=af[:], in_=f[:], func=ACT.Abs)
+            nc.scalar.activation(out=cos_t[:], in_=af[:], func=ACT.Sin, scale=-TWO_PI, bias=0.5 * math.pi)
+            nc.scalar.activation(out=sin_t[:], in_=f[:], func=ACT.Sin, scale=TWO_PI)
+            tables[t] = (cos_t, sin_t)
+
+        def turn(words):
+            tp = tps.tile([P, 2, 2, P], F32, name="tp", tag="tp")
+            for g in (0, 1):
+                for u in (0, 1):
+                    nc.tensor.transpose(tp[:, g, u, :], words[:, 256 * g + u : 256 * (g + 1) : 2], ident[:])
+            gr = grp.tile([P, 2 * HALF], BF16, name="gr", tag="gr", align_bytes=64)
+            nc.scalar.copy(
+                out=gr[:].bitcast(F32).rearrange("p (g q u) -> p g q u", g=2, u=2), in_=tp[:].rearrange("p g u q -> p g q u")
+            )
+            return gr
+
+        xc = {}
+        xs = {}
+        x_grouped = {}
+
+        def x_turn(t):
+            x_grouped[t] = turn(x_words[t])
+
+        def x_quant(t):
+            xc[t] = const.tile([P, 2 * P], U32, name="xc%d" % t, align_bytes=64)
+            xs[t] = const.tile([P, 2 * P], U8, name="xs%d" % t, align_bytes=64)
+            nc.vector.quantize_mx(out=xc[t][:].bitcast(FP8X4), scales=xs[t][:], in_=x_grouped[t][:])
+
+        wc = {}
+        ws = {}
+        for g in (0, 1):
+            for h in (0, 1):
+                wc[(g, h)] = const.tile([P, HALF], U32, name="wc%d%d" % (g, h), align_bytes=64)
+                ws[(g, h)] = const.tile([P, HALF], U8, name="ws%d%d" % (g, h), align_bytes=64)
+
+        def wprep(j):
+            grs = [turn(w_raw[j][:, h, :].bitcast(F32)) for h in (0, 1)]
+            for h in (0, 1):
+                for g in (0, 1):
+                    nc.vector.quantize_mx(
+                        out=wc[(g, h)][:, j * P : (j + 1) * P].bitcast(FP8X4),
+                        scales=ws[(g, h)][:, j * P : (j + 1) * P],
+                        in_=grs[h][:, g * HALF : (g + 1) * HALF],
+                    )
+
+        gamma_f = const.tile([P, C], F32, name="gamma_f")
+
+        def gamma_spread():
+            for h in (0, 1):
+                gp = tps.tile([P, HALF], F32, name="gp", tag="tp")
+                nc.tensor.matmul(out=gp[:], lhsT=ones_bf[:], rhs=g_row[:, h * HALF : (h + 1) * HALF], start=True, stop=True)
+                nc.scalar.copy(out=gamma_f[:, h * HALF : (h + 1) * HALF], in_=gp[:])
+
+        st = {}
+
+        def mm(t):
+            acc = [accp.tile([P, HALF], F32, name="acc%d" % h, tag="acc%d" % h) for h in (0, 1)]
+            for g in (0, 1):
+                for h in (0, 1):
+                    nc.tensor.matmul_mx(
+                        out=acc[h][:],
+                        lhsT=xc[t][:, g * P : (g + 1) * P].bitcast(FP8X4),
+                        lhsT_scale=xs[t][:, g * P : (g + 1) * P],
+                        rhs=wc[(g, h)][:].bitcast(FP8X4),
+                        rhs_scale=ws[(g, h)][:],
+                        start=(g == 0),
+                        stop=(g == 1),
+                    )
+            st[t] = {"acc": acc}
+
+        def products(t, h):
+            d = st[t]
+            if h == 0:
+                d["t1"] = work.tile([P, 2, HALF], F32, name="t1", tag="t1", bufs=2)
+                d["t2"] = work.tile([P, 2, HALF], F32, name="t2", tag="t2", bufs=2)
+                d["sums"] = stat.tile([P, 4], F32, name="sums", tag="sums")
+            k = d["acc"][h]
+            cos_t, sin_t = tables[t]
+            t1, t2, sums = d["t1"], d["t2"], d["sums"]
+            stt = nc.vector.scalar_tensor_tensor
+            if h == 0:
+                stt(out=t1[:, 0, :], in0=k[:], scalar=1.0, in1=cos_t[:], op0=ALU.mult, op1=ALU.mult, accum_out=sums[:, 0:1])
+                stt(out=t2[:, 1, :], in0=k[:], scalar=1.0, in1=sin_t[:], op0=ALU.mult, op1=ALU.mult, accum_out=sums[:, 1:2])
+            else:
+                stt(out=t2[:, 0, :], in0=k[:], scalar=-1.0, in1=sin_t[:], op0=ALU.mult, op1=ALU.mult, accum_out=sums[:, 2:3])
+                stt(out=t1[:, 1, :], in0=k[:], scalar=1.0, in1=cos_t[:], op0=ALU.mult, op1=ALU.mult, accum_out=sums[:, 3:4])
+
+        def mean(t):
+            d = st[t]
+            junk4 = stat.tile([P, 4], F32, name="junk4", tag="junk4")
+            d["negmu"] = stat.tile([P, 1], F32, name="negmu", tag="negmu")
+            nc.scalar.activation(out=junk4[:], in_=d["sums"][:], func=ACT.Identity, scale=-1.0 / C, accum_out=d["negmu"][:])
+
+        def add(t):
+            d = st[t]
+            d["rot"] = work.tile([P, C], F32, name="rot", tag="rot", bufs=1)
+            eng = nc.vector if t == LAST else nc.gpsimd
+            eng.tensor_tensor(
+                out=d["rot"][:].rearrange("p (i s) -> p i s", s=2), in0=d["t1"][:].rearrange("p s i -> p i s"),
+                in1=d["t2"][:].rearrange("p s i -> p i s"), op=ALU.add,
+            )
+
+        def variance(t):
+            d = st[t]
+            junk = work.tile([P, C], F32, name="junk", tag="junk", bufs=2)
+            ssq = stat.tile([P, 1], F32, name="ssq", tag="ssq")
+            ve = stat.tile([P, 1], F32, name="ve", tag="ve")
+            d["rstd"] = stat.tile([P, 1], F32, name="rstd", tag="rstd")
+            nc.scalar.activation(out=junk[:], in_=d["rot"][:], func=ACT.Square, bias=d["negmu"][:, 0:1], scale=1.0, accum_out=ssq[:])
+            nc.gpsimd.tensor_scalar(out=ve[:], in0=ssq[:], scalar1=1.0 / C, scalar2=EPS, op0=ALU.mult, op1=ALU.add)
+            nc.gpsimd.tensor_tensor(out=d["rstd"][:], in0=ve[:], in1=neghalf[:], op=ALU.pow)
+
+        def gain(t):
+            d = st[t]
+            d["y0"] = work.tile([P, C], F32, name="y0", tag="y0")
+            nc.vector.scalar_tensor_tensor(
+                out=d["y0"][:], in0=d["rot"][:], scalar=d["negmu"][:, 0:1], in1=gamma_f[:], op0=ALU.add, op1=ALU.mult
+            )
+
+        def scale_out(t):
+            d = st[t]
+            d["o0"] = work.tile([P, C], F32, name="o0", tag="o0")
+            o0, y0, rstd = d["o0"], d["y0"], d["rstd"]
+            if t == LAST:
+                nc.vector.tensor_scalar(out=o0[:], in0=y0[:], scalar1=rstd[:, 0:1], scalar2=None, op0=ALU.mult)
+            elif t in SCALE_ON_G:
+                nc.gpsimd.tensor_scalar(out=o0[:], in0=y0[:], scalar1=rstd[:, 0:1], scalar2=0.0, op0=ALU.mult, op1=ALU.add)
+            else:
+                nc.scalar.activation(out=o0[:], in_=y0[:], func=ACT.Copy, scale=rstd[:, 0:1])
+            nc.sync.dma_start(out=o0_view[:, t, :], in_=o0[:])
+
+        def row_max(t):
+            d = st[t]
+            d["amax_y"] = stat.tile([P, 1], F32, name="amax_y", tag="amax_y")
+            nc.vector.tensor_reduce(out=d["amax_y"][:], in_=d["y0"][:], axis=AX.X, op=ALU.max, apply_absolute_value=True)
+
+        def row_max_scaled(t):
+            d = st[t]
+            d["amax"] = stat.tile([P, 1], F32, name="amax", tag="amax")
+            nc.vector.tensor_scalar(out=d["amax"][:], in0=d["amax_y"][:], scalar1=d["rstd"][:, 0:1], scalar2=None, op0=ALU.mult)
+
+        def row_recip(t):
+            d = st[t]
+            d["ra"] = stat.tile([P, 1], F32, name="ra", tag="ra")
+            nc.vector.reciprocal(out=d["ra"][:], in_=d["amax"][:])
+
+        def cast_out(t):
+            d = st[t]
+            r = stat.tile([P, 1], F32, name="r", tag="r")
+            nc.scalar.activation(out=r[:], in_=d["ra"][:], func=ACT.Copy, scale=448.0)
+            q8 = work.tile([P, C], FP8, name="q8", tag="q8")
+            o0 = d["o0"]
+            split = HALF if t == LAST else C
+            nc.scalar.activation(
+                out=q8[:, 0:split], in_=o0[:, 0:split], func=ACT.Identity, scale=r[:, 0:1], bias=zeros[:, 0:1], saturate=False
+            )
+            if split < C:
+                nc.vector.tensor_scalar(
+                    out=q8[:, split:C], in0=o0[:, split:C], scalar1=r[:, 0:1], scalar2=None, op0=ALU.mult, saturate=False
+                )
+            nc.sync.dma_start(out=o1_view[:, t, :], in_=q8[:].bitcast(U8))
+
+        x_turn(0)
+        for t in range(NT):
+            rr(t)
+        trig_tile(0)
+        x_quant(0)
+        wprep(0)
+        wprep(1)
+        trig_tile(1)
+        wprep(2)
+        wprep(3)
+        x_turn(1)
+        x_quant(1)
+        x_turn(2)
+        mm(0)
+        mm(1)
+        gamma_spread()
+
+        for t in range(NT + 2):
+            if 0 <= t - 1 < NT:
+                add(t - 1)
+            if t < NT:
+                products(t, 0)
+            if 0 <= t - 2 < NT:
+                row_max(t - 2)
+            if t < NT:
+                products(t, 1)
+            if 0 <= t - 2 < NT:
+                scale_out(t - 2)
+            if t + 2 < NT:
+                trig_tile(t + 2)
+            if 0 <= t - 1 < NT:
+                variance(t - 1)
+            if t < NT:
+                mean(t)
+            if 0 <= t - 2 < NT:
+                row_max_scaled(t - 2)
+            if t + 2 < NT:
+                x_quant(t + 2)
+                mm(t + 2)
+            if 0 <= t - 2 < NT:
+                row_recip(t - 2)
+                cast_out(t - 2)
+            if t + 3 < NT:
+                x_turn(t + 3)
+            if 0 <= t - 1 < NT:
+                gain(t - 1)

@@ -34,7 +34,7 @@ def tile_attentionalsplatting_pa_kernel(tc, tokens, tracks, w_k, k_gamma, out_0,
     nc = tc.nc
     x_view = tokens.flatten_outer_dims().rearrange("(p t) k -> p t k", t=NT)
     pos_view = tracks.flatten_outer_dims().rearrange("(p t) c -> p (t c)", t=NT)
-    w_view = w_k.rearrange("(j q h) k -> j q (h k)", j=4, h=2)
+    w_view = w_k.rearrange("(a b q h) k -> h a q b k", a=2, b=2, h=2)
     g_view = k_gamma.rearrange("(o c) -> o c", o=1)
     o0_view = out_0.flatten_outer_dims().rearrange("(p t) c -> p t c", t=NT)
     o1_view = out_1.flatten_outer_dims().rearrange("(p t) c -> p t c", t=NT)
@@ -76,11 +76,12 @@ def tile_attentionalsplatting_pa_kernel(tc, tokens, tracks, w_k, k_gamma, out_0,
                 x_words[t] = xr[:, t - a, :].bitcast(F32)
 
         load_x(*X_CHUNKS[0])
-        w_raw = []
-        for j in range(4):
-            wr = const.tile([P, 2, K], BF16, name="wr%d" % j)
-            nc.sync.dma_start(out=wr[:].rearrange("q h k -> q (h k)"), in_=w_view[j])
-            w_raw.append(wr)
+        w_raw = {}
+        for h in (0, 1):
+            for a in (0, 1):
+                wr = const.tile([P, 2, K], BF16, name="wr%d%d" % (h, a))
+                nc.sync.dma_start(out=wr[:], in_=w_view[h, a])
+                w_raw[(h, a)] = wr
         for a, b in X_CHUNKS[1:]:
             load_x(a, b)
         nc.scalar.dma_start(out=g_row[0:1, :], in_=g_view)
@@ -123,11 +124,11 @@ def tile_attentionalsplatting_pa_kernel(tc, tokens, tracks, w_k, k_gamma, out_0,
             nc.scalar.activation(out=sin_t[:], in_=f[:], func=ACT.Sin, scale=TWO_PI)
             tables[t] = (cos_t, sin_t)
 
-        def turn(words):
+        def turn(word_runs):
             tp = tps.tile([P, 2, 2, P], F32, name="tp", tag="tp")
             for g in (0, 1):
                 for u in (0, 1):
-                    nc.tensor.transpose(tp[:, g, u, :], words[:, 256 * g + u : 256 * (g + 1) : 2], ident[:])
+                    nc.tensor.transpose(tp[:, g, u, :], word_runs[g][:, u : 2 * P : 2], ident[:])
             gr = grp.tile([P, 2 * HALF], BF16, name="gr", tag="gr", align_bytes=64)
             nc.scalar.copy(
                 out=gr[:].bitcast(F32).rearrange("p (g q u) -> p g q u", g=2, u=2), in_=tp[:].rearrange("p g u q -> p g q u")
@@ -139,7 +140,7 @@ def tile_attentionalsplatting_pa_kernel(tc, tokens, tracks, w_k, k_gamma, out_0,
         x_grouped = {}
 
         def x_turn(t):
-            x_grouped[t] = turn(x_words[t])
+            x_grouped[t] = turn([x_words[t][:, 256 * g : 256 * (g + 1)] for g in (0, 1)])
 
         def x_quant(t):
             xc[t] = const.tile([P, 2 * P], U32, name="xc%d" % t, align_bytes=64)
@@ -153,15 +154,15 @@ def tile_attentionalsplatting_pa_kernel(tc, tokens, tracks, w_k, k_gamma, out_0,
                 wc[(g, h)] = const.tile([P, HALF], U32, name="wc%d%d" % (g, h), align_bytes=64)
                 ws[(g, h)] = const.tile([P, HALF], U8, name="ws%d%d" % (g, h), align_bytes=64)
 
-        def wprep(j):
-            grs = [turn(w_raw[j][:, h, :].bitcast(F32)) for h in (0, 1)]
-            for h in (0, 1):
-                for g in (0, 1):
-                    nc.vector.quantize_mx(
-                        out=wc[(g, h)][:, j * P : (j + 1) * P].bitcast(FP8X4),
-                        scales=ws[(g, h)][:, j * P : (j + 1) * P],
-                        in_=grs[h][:, g * HALF : (g + 1) * HALF],
-                    )
+        def wprep(h, a):
+            wr = w_raw[(h, a)]
+            grs = [turn([wr[:, b, :].bitcast(F32)[:, 256 * g : 256 * (g + 1)] for b in (0, 1)]) for g in (0, 1)]
+            for g in (0, 1):
+                nc.vector.quantize_mx(
+                    out=wc[(g, h)][:, a * 2 * P : (a + 1) * 2 * P].bitcast(FP8X4),
+                    scales=ws[(g, h)][:, a * 2 * P : (a + 1) * 2 * P],
+                    in_=grs[g][:],
+                )
 
         gamma_f = const.tile([P, C], F32, name="gamma_f")
 
@@ -175,8 +176,8 @@ def tile_attentionalsplatting_pa_kernel(tc, tokens, tracks, w_k, k_gamma, out_0,
 
         def mm(t):
             acc = [accp.tile([P, HALF], F32, name="acc%d" % h, tag="acc%d" % h) for h in (0, 1)]
-            for g in (0, 1):
-                for h in (0, 1):
+            for h in (0, 1):
+                for g in (0, 1):
                     nc.tensor.matmul_mx(
                         out=acc[h][:],
                         lhsT=xc[t][:, g * P : (g + 1) * P].bitcast(FP8X4),
@@ -216,8 +217,8 @@ def tile_attentionalsplatting_pa_kernel(tc, tokens, tracks, w_k, k_gamma, out_0,
             d["rot"] = work.tile([P, C], F32, name="rot", tag="rot", bufs=1)
             eng = nc.vector if t == LAST else nc.gpsimd
             eng.tensor_tensor(
-                out=d["rot"][:].rearrange("p (i s) -> p i s", s=2), in0=d["t1"][:].rearrange("p s i -> p i s"),
-                in1=d["t2"][:].rearrange("p s i -> p i s"), op=ALU.add,
+                out=d["rot"][:], in0=d["t1"][:].rearrange("p s i -> p (s i)"),
+                in1=d["t2"][:].rearrange("p s i -> p (s i)"), op=ALU.add,
             )
 
         def variance(t):
@@ -234,7 +235,8 @@ def tile_attentionalsplatting_pa_kernel(tc, tokens, tracks, w_k, k_gamma, out_0,
             d = st[t]
             d["y0"] = work.tile([P, C], F32, name="y0", tag="y0")
             nc.vector.scalar_tensor_tensor(
-                out=d["y0"][:], in0=d["rot"][:], scalar=d["negmu"][:, 0:1], in1=gamma_f[:], op0=ALU.add, op1=ALU.mult
+                out=d["y0"][:].rearrange("p (i s) -> p i s", s=2), in0=d["rot"][:].rearrange("p (s i) -> p i s", s=2),
+                scalar=d["negmu"][:, 0:1], in1=gamma_f[:].rearrange("p (i s) -> p i s", s=2), op0=ALU.add, op1=ALU.mult,
             )
 
         def scale_out(t):
@@ -285,11 +287,11 @@ def tile_attentionalsplatting_pa_kernel(tc, tokens, tracks, w_k, k_gamma, out_0,
             rr(t)
         trig_tile(0)
         x_quant(0)
-        wprep(0)
-        wprep(1)
+        wprep(0, 0)
+        wprep(0, 1)
         trig_tile(1)
-        wprep(2)
-        wprep(3)
+        wprep(1, 0)
+        wprep(1, 1)
         x_turn(1)
         x_quant(1)
         x_turn(2)

@@ -26,7 +26,7 @@ EPS = 1e-6
 TWO_PI = 2.0 * math.pi
 RATIO = 100.0 ** (-1.0 / 256.0)
 LAST = NT - 1
-SCALE_ON_G = (1, 3, 5)
+SCALE_ON_G = (0, 1, 2, 3, 4, 5, 6)
 X_CHUNKS = ((0, 1), (1, 2), (2, 4), (4, 8))
 
 
@@ -46,7 +46,8 @@ def tile_attentionalsplatting_pa_kernel(tc, tokens, tracks, w_k, k_gamma, out_0,
         trig = ctx.enter_context(tc.tile_pool(name="trig", bufs=4))
         work = ctx.enter_context(tc.tile_pool(name="work", bufs=3))
         stat = ctx.enter_context(tc.tile_pool(name="stat", bufs=4))
-        tps = ctx.enter_context(tc.psum_pool(name="tps", bufs=4))
+        tps = ctx.enter_context(tc.psum_pool(name="tps", bufs=2))
+        gps = ctx.enter_context(tc.psum_pool(name="gps", bufs=1))
         accp = ctx.enter_context(tc.psum_pool(name="accp", bufs=2))
         ctx.enter_context(tc.manual_schedule())
 
@@ -124,8 +125,11 @@ def tile_attentionalsplatting_pa_kernel(tc, tokens, tracks, w_k, k_gamma, out_0,
             nc.scalar.activation(out=sin_t[:], in_=f[:], func=ACT.Sin, scale=TWO_PI)
             tables[t] = (cos_t, sin_t)
 
-        def turn(word_runs):
-            tp = tps.tile([P, 2, 2, P], F32, name="tp", tag="tp")
+        def turn(word_runs, bank=None):
+            if bank is None:
+                tp = tps.tile([P, 2, 2, P], F32, name="tp", tag="tp")
+            else:
+                tp = accp.tile([P, 2, 2, P], F32, name="tp_" + bank, tag=bank)
             for g in (0, 1):
                 for u in (0, 1):
                     nc.tensor.transpose(tp[:, g, u, :], word_runs[g][:, u : 2 * P : 2], ident[:])
@@ -156,7 +160,8 @@ def tile_attentionalsplatting_pa_kernel(tc, tokens, tracks, w_k, k_gamma, out_0,
 
         def wprep(h, a):
             wr = w_raw[(h, a)]
-            grs = [turn([wr[:, b, :].bitcast(F32)[:, 256 * g : 256 * (g + 1)] for b in (0, 1)]) for g in (0, 1)]
+            banks = ("acc0", "acc1") if a == 1 else (None, None)
+            grs = [turn([wr[:, b, :].bitcast(F32)[:, 256 * g : 256 * (g + 1)] for b in (0, 1)], banks[g]) for g in (0, 1)]
             for g in (0, 1):
                 nc.vector.quantize_mx(
                     out=wc[(g, h)][:, a * 2 * P : (a + 1) * 2 * P].bitcast(FP8X4),
@@ -164,13 +169,13 @@ def tile_attentionalsplatting_pa_kernel(tc, tokens, tracks, w_k, k_gamma, out_0,
                     in_=grs[g][:],
                 )
 
-        gamma_f = const.tile([P, C], F32, name="gamma_f")
+        gamma_ps = [gps.tile([P, HALF], F32, name="gamma_ps%d" % b) for b in (0, 1)]
 
         def gamma_spread():
-            for h in (0, 1):
-                gp = tps.tile([P, HALF], F32, name="gp", tag="tp")
-                nc.tensor.matmul(out=gp[:], lhsT=ones_bf[:], rhs=g_row[:, h * HALF : (h + 1) * HALF], start=True, stop=True)
-                nc.scalar.copy(out=gamma_f[:, h * HALF : (h + 1) * HALF], in_=gp[:])
+            for b in (0, 1):
+                nc.tensor.matmul(
+                    out=gamma_ps[b][:], lhsT=ones_bf[:], rhs=g_row[:, b * HALF : (b + 1) * HALF], start=True, stop=True
+                )
 
         st = {}
 
@@ -189,7 +194,7 @@ def tile_attentionalsplatting_pa_kernel(tc, tokens, tracks, w_k, k_gamma, out_0,
                     )
             st[t] = {"acc": acc}
 
-        def products(t, h):
+        def products(t, h, parts=(0, 1)):
             d = st[t]
             if h == 0:
                 d["t1"] = work.tile([P, 2, HALF], F32, name="t1", tag="t1", bufs=2)
@@ -202,8 +207,9 @@ def tile_attentionalsplatting_pa_kernel(tc, tokens, tracks, w_k, k_gamma, out_0,
             if h == 0:
                 stt(out=t1[:, 0, :], in0=k[:], scalar=1.0, in1=cos_t[:], op0=ALU.mult, op1=ALU.mult, accum_out=sums[:, 0:1])
                 stt(out=t2[:, 1, :], in0=k[:], scalar=1.0, in1=sin_t[:], op0=ALU.mult, op1=ALU.mult, accum_out=sums[:, 1:2])
-            else:
+            if h == 1 and 0 in parts:
                 stt(out=t2[:, 0, :], in0=k[:], scalar=-1.0, in1=sin_t[:], op0=ALU.mult, op1=ALU.mult, accum_out=sums[:, 2:3])
+            if h == 1 and 1 in parts:
                 stt(out=t1[:, 1, :], in0=k[:], scalar=1.0, in1=cos_t[:], op0=ALU.mult, op1=ALU.mult, accum_out=sums[:, 3:4])
 
         def mean(t):
@@ -214,7 +220,7 @@ def tile_attentionalsplatting_pa_kernel(tc, tokens, tracks, w_k, k_gamma, out_0,
 
         def add(t):
             d = st[t]
-            d["rot"] = work.tile([P, C], F32, name="rot", tag="rot", bufs=1)
+            d["rot"] = work.tile([P, C], F32, name="rot", tag="rot", bufs=2)
             eng = nc.vector if t == LAST else nc.gpsimd
             eng.tensor_tensor(
                 out=d["rot"][:], in0=d["t1"][:].rearrange("p s i -> p (s i)"),
@@ -234,10 +240,13 @@ def tile_attentionalsplatting_pa_kernel(tc, tokens, tracks, w_k, k_gamma, out_0,
         def gain(t):
             d = st[t]
             d["y0"] = work.tile([P, C], F32, name="y0", tag="y0")
-            nc.vector.scalar_tensor_tensor(
-                out=d["y0"][:].rearrange("p (i s) -> p i s", s=2), in0=d["rot"][:].rearrange("p (s i) -> p i s", s=2),
-                scalar=d["negmu"][:, 0:1], in1=gamma_f[:].rearrange("p (i s) -> p i s", s=2), op0=ALU.add, op1=ALU.mult,
-            )
+            rot_pairs = d["rot"][:].rearrange("p (s i) -> p i s", s=2)
+            for b in (0, 1):
+                nc.vector.scalar_tensor_tensor(
+                    out=d["y0"][:, b * HALF : (b + 1) * HALF].rearrange("p (i s) -> p i s", s=2),
+                    in0=rot_pairs[:, b * 256 : (b + 1) * 256, :], scalar=d["negmu"][:, 0:1],
+                    in1=gamma_ps[b][:].rearrange("p (i s) -> p i s", s=2), op0=ALU.add, op1=ALU.mult,
+                )
 
         def scale_out(t):
             d = st[t]
@@ -300,22 +309,18 @@ def tile_attentionalsplatting_pa_kernel(tc, tokens, tracks, w_k, k_gamma, out_0,
         gamma_spread()
 
         for t in range(NT + 2):
-            if 0 <= t - 1 < NT:
-                add(t - 1)
             if t < NT:
                 products(t, 0)
-            if 0 <= t - 2 < NT:
-                row_max(t - 2)
-            if t < NT:
-                products(t, 1)
             if 0 <= t - 2 < NT:
                 scale_out(t - 2)
             if t + 2 < NT:
                 trig_tile(t + 2)
+            if 0 <= t - 2 < NT:
+                row_max(t - 2)
             if 0 <= t - 1 < NT:
                 variance(t - 1)
             if t < NT:
-                mean(t)
+                products(t, 1, (0,))
             if 0 <= t - 2 < NT:
                 row_max_scaled(t - 2)
             if t + 2 < NT:
@@ -323,7 +328,13 @@ def tile_attentionalsplatting_pa_kernel(tc, tokens, tracks, w_k, k_gamma, out_0,
                 mm(t + 2)
             if 0 <= t - 2 < NT:
                 row_recip(t - 2)
+            if t < NT:
+                products(t, 1, (1,))
+                add(t)
+            if 0 <= t - 2 < NT:
                 cast_out(t - 2)
+            if t < NT:
+                mean(t)
             if t + 3 < NT:
                 x_turn(t + 3)
             if 0 <= t - 1 < NT:

@@ -46,7 +46,7 @@ def tile_attentionalsplatting_pa_kernel(tc, tokens, tracks, w_k, k_gamma, out_0,
         trig = ctx.enter_context(tc.tile_pool(name="trig", bufs=4))
         work = ctx.enter_context(tc.tile_pool(name="work", bufs=3))
         stat = ctx.enter_context(tc.tile_pool(name="stat", bufs=4))
-        tps = ctx.enter_context(tc.psum_pool(name="tps", bufs=2))
+        tps = ctx.enter_context(tc.psum_pool(name="tps", bufs=3))
         gps = ctx.enter_context(tc.psum_pool(name="gps", bufs=1))
         accp = ctx.enter_context(tc.psum_pool(name="accp", bufs=2))
         ctx.enter_context(tc.manual_schedule())
@@ -169,12 +169,13 @@ def tile_attentionalsplatting_pa_kernel(tc, tokens, tracks, w_k, k_gamma, out_0,
                     in_=grs[g][:],
                 )
 
-        gamma_ps = [gps.tile([P, HALF], F32, name="gamma_ps%d" % b) for b in (0, 1)]
+        gamma_ps = gps.tile([P, C], BF16, name="gamma_ps")
 
         def gamma_spread():
             for b in (0, 1):
                 nc.tensor.matmul(
-                    out=gamma_ps[b][:], lhsT=ones_bf[:], rhs=g_row[:, b * HALF : (b + 1) * HALF], start=True, stop=True
+                    out=gamma_ps[:, b * HALF : (b + 1) * HALF], lhsT=ones_bf[:], rhs=g_row[:, b * HALF : (b + 1) * HALF],
+                    start=True, stop=True,
                 )
 
         st = {}
@@ -240,13 +241,10 @@ def tile_attentionalsplatting_pa_kernel(tc, tokens, tracks, w_k, k_gamma, out_0,
         def gain(t):
             d = st[t]
             d["y0"] = work.tile([P, C], F32, name="y0", tag="y0")
-            rot_pairs = d["rot"][:].rearrange("p (s i) -> p i s", s=2)
-            for b in (0, 1):
-                nc.vector.scalar_tensor_tensor(
-                    out=d["y0"][:, b * HALF : (b + 1) * HALF].rearrange("p (i s) -> p i s", s=2),
-                    in0=rot_pairs[:, b * 256 : (b + 1) * 256, :], scalar=d["negmu"][:, 0:1],
-                    in1=gamma_ps[b][:].rearrange("p (i s) -> p i s", s=2), op0=ALU.add, op1=ALU.mult,
-                )
+            nc.vector.scalar_tensor_tensor(
+                out=d["y0"][:].rearrange("p (i s) -> p i s", s=2), in0=d["rot"][:].rearrange("p (s i) -> p i s", s=2),
+                scalar=d["negmu"][:, 0:1], in1=gamma_ps[:].rearrange("p (i s) -> p i s", s=2), op0=ALU.add, op1=ALU.mult,
+            )
 
         def scale_out(t):
             d = st[t]
@@ -268,7 +266,9 @@ def tile_attentionalsplatting_pa_kernel(tc, tokens, tracks, w_k, k_gamma, out_0,
         def row_max_scaled(t):
             d = st[t]
             d["amax"] = stat.tile([P, 1], F32, name="amax", tag="amax")
-            nc.vector.tensor_scalar(out=d["amax"][:], in0=d["amax_y"][:], scalar1=d["rstd"][:, 0:1], scalar2=None, op0=ALU.mult)
+            nc.vector.tensor_scalar(
+                out=d["amax"][:], in0=d["amax_y"][:], scalar1=d["rstd"][:, 0:1], scalar2=1.0 / 448.0, op0=ALU.mult, op1=ALU.mult
+            )
 
         def row_recip(t):
             d = st[t]
@@ -277,8 +277,7 @@ def tile_attentionalsplatting_pa_kernel(tc, tokens, tracks, w_k, k_gamma, out_0,
 
         def cast_out(t):
             d = st[t]
-            r = stat.tile([P, 1], F32, name="r", tag="r")
-            nc.scalar.activation(out=r[:], in_=d["ra"][:], func=ACT.Copy, scale=448.0)
+            r = d["ra"]
             q8 = work.tile([P, C], FP8, name="q8", tag="q8")
             o0 = d["o0"]
             split = HALF if t == LAST else C

@@ -118,12 +118,11 @@ def tile_attentionalsplatting_pa_kernel(tc, tokens, tracks, w_k, k_gamma, out_0,
         def trig_tile(t):
             f = fracs[t]
             af = work.tile([P, HALF], F32, name="af", tag="af", bufs=2)
-            sin_t = trig.tile([P, HALF], F32, name="sin_t", tag="sin_t")
-            cos_t = trig.tile([P, HALF], F32, name="cos_t", tag="cos_t")
+            cos_sin = trig.tile([P, 2, HALF], F32, name="cos_sin", tag="cos_sin")
             nc.scalar.activation(out=af[:], in_=f[:], func=ACT.Abs)
-            nc.scalar.activation(out=cos_t[:], in_=af[:], func=ACT.Sin, scale=-TWO_PI, bias=0.5 * math.pi)
-            nc.scalar.activation(out=sin_t[:], in_=f[:], func=ACT.Sin, scale=TWO_PI)
-            tables[t] = (cos_t, sin_t)
+            nc.scalar.activation(out=cos_sin[:, 0, :], in_=af[:], func=ACT.Sin, scale=-TWO_PI, bias=0.5 * math.pi)
+            nc.scalar.activation(out=cos_sin[:, 1, :], in_=f[:], func=ACT.Sin, scale=TWO_PI)
+            tables[t] = cos_sin
 
         def turn(word_runs, bank=None):
             if bank is None:
@@ -200,24 +199,34 @@ def tile_attentionalsplatting_pa_kernel(tc, tokens, tracks, w_k, k_gamma, out_0,
             if h == 0:
                 d["t1"] = work.tile([P, 2, HALF], F32, name="t1", tag="t1", bufs=2)
                 d["t2"] = work.tile([P, 2, HALF], F32, name="t2", tag="t2", bufs=2)
-                d["sums"] = stat.tile([P, 4], F32, name="sums", tag="sums")
+                d["sums"] = stat.tile([P, 3], F32, name="sums", tag="sums")
             k = d["acc"][h]
-            cos_t, sin_t = tables[t]
+            cos_sin = tables[t]
             t1, t2, sums = d["t1"], d["t2"], d["sums"]
             stt = nc.vector.scalar_tensor_tensor
             if h == 0:
-                stt(out=t1[:, 0, :], in0=k[:], scalar=1.0, in1=cos_t[:], op0=ALU.mult, op1=ALU.mult, accum_out=sums[:, 0:1])
-                stt(out=t2[:, 1, :], in0=k[:], scalar=1.0, in1=sin_t[:], op0=ALU.mult, op1=ALU.mult, accum_out=sums[:, 1:2])
+                stt(
+                    out=t1[:], in0=k[:].unsqueeze(1).to_broadcast([P, 2, HALF]), scalar=1.0, in1=cos_sin[:],
+                    op0=ALU.mult, op1=ALU.mult, accum_out=sums[:, 0:1],
+                )
             if h == 1 and 0 in parts:
-                stt(out=t2[:, 0, :], in0=k[:], scalar=-1.0, in1=sin_t[:], op0=ALU.mult, op1=ALU.mult, accum_out=sums[:, 2:3])
+                stt(
+                    out=t2[:, 0, :], in0=k[:], scalar=-1.0, in1=cos_sin[:, 1, :], op0=ALU.mult, op1=ALU.mult,
+                    accum_out=sums[:, 1:2],
+                )
             if h == 1 and 1 in parts:
-                stt(out=t1[:, 1, :], in0=k[:], scalar=1.0, in1=cos_t[:], op0=ALU.mult, op1=ALU.mult, accum_out=sums[:, 3:4])
+                stt(
+                    out=t2[:, 1, :], in0=k[:], scalar=1.0, in1=cos_sin[:, 0, :], op0=ALU.mult, op1=ALU.mult,
+                    accum_out=sums[:, 2:3],
+                )
 
         def mean(t):
             d = st[t]
-            junk4 = stat.tile([P, 4], F32, name="junk4", tag="junk4")
+            junk4 = stat.tile([P, 3], F32, name="junk4", tag="junk4")
             d["negmu"] = stat.tile([P, 1], F32, name="negmu", tag="negmu")
-            nc.scalar.activation(out=junk4[:], in_=d["sums"][:], func=ACT.Identity, scale=-1.0 / C, accum_out=d["negmu"][:])
+            nc.vector.tensor_scalar(
+                out=junk4[:], in0=d["sums"][:], scalar1=-1.0 / C, scalar2=None, op0=ALU.mult, op1=ALU.add, accum_out=d["negmu"][:]
+            )
 
         def add(t):
             d = st[t]
@@ -250,9 +259,7 @@ def tile_attentionalsplatting_pa_kernel(tc, tokens, tracks, w_k, k_gamma, out_0,
             d = st[t]
             d["o0"] = work.tile([P, C], F32, name="o0", tag="o0")
             o0, y0, rstd = d["o0"], d["y0"], d["rstd"]
-            if t == LAST:
-                nc.vector.tensor_scalar(out=o0[:], in0=y0[:], scalar1=rstd[:, 0:1], scalar2=None, op0=ALU.mult)
-            elif t in SCALE_ON_G:
+            if t in SCALE_ON_G:
                 nc.gpsimd.tensor_scalar(out=o0[:], in0=y0[:], scalar1=rstd[:, 0:1], scalar2=0.0, op0=ALU.mult, op1=ALU.add)
             else:
                 nc.scalar.activation(out=o0[:], in_=y0[:], func=ACT.Copy, scale=rstd[:, 0:1])
@@ -280,7 +287,7 @@ def tile_attentionalsplatting_pa_kernel(tc, tokens, tracks, w_k, k_gamma, out_0,
             r = d["ra"]
             q8 = work.tile([P, C], FP8, name="q8", tag="q8")
             o0 = d["o0"]
-            split = HALF if t == LAST else C
+            split = 384 if t == LAST else C
             nc.scalar.activation(
                 out=q8[:, 0:split], in_=o0[:, 0:split], func=ACT.Identity, scale=r[:, 0:1], bias=zeros[:, 0:1], saturate=False
             )
@@ -332,9 +339,9 @@ def tile_attentionalsplatting_pa_kernel(tc, tokens, tracks, w_k, k_gamma, out_0,
                 add(t)
             if 0 <= t - 2 < NT:
                 cast_out(t - 2)
-            if t < NT:
-                mean(t)
             if t + 3 < NT:
                 x_turn(t + 3)
             if 0 <= t - 1 < NT:
                 gain(t - 1)
+            if t < NT:
+                mean(t)

@@ -124,7 +124,7 @@ def tile_attentionalsplatting_pa_kernel(tc, tokens, tracks, w_k, k_gamma, out_0,
             nc.scalar.activation(out=cos_sin[:, 1, :], in_=f[:], func=ACT.Sin, scale=TWO_PI)
             tables[t] = cos_sin
 
-        def turn(word_runs, bank=None):
+        def turn(word_runs, bank=None, grouped=None):
             if bank is None:
                 tp = tps.tile([P, 2, 2, P], F32, name="tp", tag="tp")
             else:
@@ -132,9 +132,11 @@ def tile_attentionalsplatting_pa_kernel(tc, tokens, tracks, w_k, k_gamma, out_0,
             for g in (0, 1):
                 for u in (0, 1):
                     nc.tensor.transpose(tp[:, g, u, :], word_runs[g][:, u : 2 * P : 2], ident[:])
-            gr = grp.tile([P, 2 * HALF], BF16, name="gr", tag="gr", align_bytes=64)
+            gr = grouped
+            if gr is None:
+                gr = grp.tile([P, 2 * HALF], BF16, name="gr", tag="gr", align_bytes=64)[:]
             nc.scalar.copy(
-                out=gr[:].bitcast(F32).rearrange("p (g q u) -> p g q u", g=2, u=2), in_=tp[:].rearrange("p g u q -> p g q u")
+                out=gr.bitcast(F32).rearrange("p (g q u) -> p g q u", g=2, u=2), in_=tp[:].rearrange("p g u q -> p g q u")
             )
             return gr
 
@@ -148,7 +150,7 @@ def tile_attentionalsplatting_pa_kernel(tc, tokens, tracks, w_k, k_gamma, out_0,
         def x_quant(t):
             xc[t] = const.tile([P, 2 * P], U32, name="xc%d" % t, align_bytes=64)
             xs[t] = const.tile([P, 2 * P], U8, name="xs%d" % t, align_bytes=64)
-            nc.vector.quantize_mx(out=xc[t][:].bitcast(FP8X4), scales=xs[t][:], in_=x_grouped[t][:])
+            nc.vector.quantize_mx(out=xc[t][:].bitcast(FP8X4), scales=xs[t][:], in_=x_grouped[t])
 
         wc = {}
         ws = {}
@@ -157,16 +159,21 @@ def tile_attentionalsplatting_pa_kernel(tc, tokens, tracks, w_k, k_gamma, out_0,
                 wc[(g, h)] = const.tile([P, HALF], U32, name="wc%d%d" % (g, h), align_bytes=64)
                 ws[(g, h)] = const.tile([P, HALF], U8, name="ws%d%d" % (g, h), align_bytes=64)
 
+        w_grouped = {}
+
         def wprep(h, a):
             wr = w_raw[(h, a)]
             banks = ("acc0", "acc1") if a == 1 else (None, None)
-            grs = [turn([wr[:, b, :].bitcast(F32)[:, 256 * g : 256 * (g + 1)] for b in (0, 1)], banks[g]) for g in (0, 1)]
             for g in (0, 1):
-                nc.vector.quantize_mx(
-                    out=wc[(g, h)][:, a * 2 * P : (a + 1) * 2 * P].bitcast(FP8X4),
-                    scales=ws[(g, h)][:, a * 2 * P : (a + 1) * 2 * P],
-                    in_=grs[g][:],
+                if a == 0:
+                    w_grouped[(g, h)] = const.tile([P, 4 * HALF], BF16, name="wg%d%d" % (g, h), align_bytes=64)
+                turn(
+                    [wr[:, b, :].bitcast(F32)[:, 256 * g : 256 * (g + 1)] for b in (0, 1)], banks[g],
+                    w_grouped[(g, h)][:, a * 2 * HALF : (a + 1) * 2 * HALF],
                 )
+            if a == 1:
+                for g in (0, 1):
+                    nc.vector.quantize_mx(out=wc[(g, h)][:].bitcast(FP8X4), scales=ws[(g, h)][:], in_=w_grouped[(g, h)][:])
 
         gamma_ps = gps.tile([P, C], BF16, name="gamma_ps")
 
@@ -224,9 +231,7 @@ def tile_attentionalsplatting_pa_kernel(tc, tokens, tracks, w_k, k_gamma, out_0,
             d = st[t]
             junk4 = stat.tile([P, 3], F32, name="junk4", tag="junk4")
             d["negmu"] = stat.tile([P, 1], F32, name="negmu", tag="negmu")
-            nc.vector.tensor_scalar(
-                out=junk4[:], in0=d["sums"][:], scalar1=-1.0 / C, scalar2=None, op0=ALU.mult, op1=ALU.add, accum_out=d["negmu"][:]
-            )
+            nc.scalar.activation(out=junk4[:], in_=d["sums"][:], func=ACT.Identity, scale=-1.0 / C, accum_out=d["negmu"][:])
 
         def add(t):
             d = st[t]
@@ -339,9 +344,9 @@ def tile_attentionalsplatting_pa_kernel(tc, tokens, tracks, w_k, k_gamma, out_0,
                 add(t)
             if 0 <= t - 2 < NT:
                 cast_out(t - 2)
+            if t < NT:
+                mean(t)
             if t + 3 < NT:
                 x_turn(t + 3)
             if 0 <= t - 1 < NT:
                 gain(t - 1)
-            if t < NT:
-                mean(t)

@@ -100,14 +100,20 @@ def tile_attentionalsplatting_pa_kernel(tc, tokens, tracks, w_k, k_gamma, out_0,
         fracs = {}
         tables = {}
 
-        def rr(t):
+        turns = {}
+
+        def rr_round(t):
             n_i = rrp.tile([P, HALF], I32, name="n_i", tag="n_i")
-            f = rrp.tile([P, HALF], F32, name="f", tag="f")
             for c in (0, 1):
                 nc.vector.tensor_scalar(
                     out=n_i[:, 256 * c : 256 * (c + 1)], in0=theta[:], scalar1=pos_f[:, 2 * t + c : 2 * t + c + 1],
                     scalar2=None, op0=ALU.mult,
                 )
+            turns[t] = n_i
+
+        def rr_frac(t):
+            n_i = turns[t]
+            f = rrp.tile([P, HALF], F32, name="f", tag="f")
             for c in (0, 1):
                 nc.vector.scalar_tensor_tensor(
                     out=f[:, 256 * c : 256 * (c + 1)], in0=theta[:], scalar=pos_f[:, 2 * t + c : 2 * t + c + 1],
@@ -145,12 +151,29 @@ def tile_attentionalsplatting_pa_kernel(tc, tokens, tracks, w_k, k_gamma, out_0,
         x_grouped = {}
 
         def x_turn(t):
-            x_grouped[t] = turn([x_words[t][:, 256 * g : 256 * (g + 1)] for g in (0, 1)])
+            runs = [x_words[t][:, 256 * g : 256 * (g + 1)] for g in (0, 1)]
+            if t < 2:
+                x_grouped[t] = turn(runs)
+            else:
+                if t % 2 == 0:
+                    x_grouped[t] = grp.tile([P, 4 * HALF], BF16, name="gr2", tag="gr2", bufs=2, align_bytes=64)
+                    x_grouped[t + 1] = x_grouped[t]
+                turn(runs, None, x_grouped[t][:, (t % 2) * 2 * HALF : (t % 2 + 1) * 2 * HALF])
 
         def x_quant(t):
-            xc[t] = const.tile([P, 2 * P], U32, name="xc%d" % t, align_bytes=64)
-            xs[t] = const.tile([P, 2 * P], U8, name="xs%d" % t, align_bytes=64)
-            nc.vector.quantize_mx(out=xc[t][:].bitcast(FP8X4), scales=xs[t][:], in_=x_grouped[t])
+            codes = const.tile([P, 2 * P], U32, name="xc%d" % t, align_bytes=64)
+            scales = const.tile([P, 2 * P], U8, name="xs%d" % t, align_bytes=64)
+            nc.vector.quantize_mx(out=codes[:].bitcast(FP8X4), scales=scales[:], in_=x_grouped[t])
+            xc[t] = codes[:]
+            xs[t] = scales[:]
+
+        def x_quant_pair(t):
+            codes = const.tile([P, 4 * P], U32, name="xc%d" % t, align_bytes=64)
+            scales = const.tile([P, 4 * P], U8, name="xs%d" % t, align_bytes=64)
+            nc.vector.quantize_mx(out=codes[:].bitcast(FP8X4), scales=scales[:], in_=x_grouped[t][:])
+            for e in (0, 1):
+                xc[t + e] = codes[:, e * 2 * P : (e + 1) * 2 * P]
+                xs[t + e] = scales[:, e * 2 * P : (e + 1) * 2 * P]
 
         wc = {}
         ws = {}
@@ -249,7 +272,7 @@ def tile_attentionalsplatting_pa_kernel(tc, tokens, tracks, w_k, k_gamma, out_0,
             ve = stat.tile([P, 1], F32, name="ve", tag="ve")
             d["rstd"] = stat.tile([P, 1], F32, name="rstd", tag="rstd")
             nc.scalar.activation(out=junk[:], in_=d["rot"][:], func=ACT.Square, bias=d["negmu"][:, 0:1], scale=1.0, accum_out=ssq[:])
-            nc.gpsimd.tensor_scalar(out=ve[:], in0=ssq[:], scalar1=1.0 / C, scalar2=EPS, op0=ALU.mult, op1=ALU.add)
+            nc.scalar.activation(out=ve[:], in_=ssq[:], func=ACT.Copy, scale=1.0 / C, bias=EPS)
             nc.gpsimd.tensor_tensor(out=d["rstd"][:], in0=ve[:], in1=neghalf[:], op=ALU.pow)
 
         def gain(t):
@@ -303,8 +326,11 @@ def tile_attentionalsplatting_pa_kernel(tc, tokens, tracks, w_k, k_gamma, out_0,
             nc.sync.dma_start(out=o1_view[:, t, :], in_=q8[:].bitcast(U8))
 
         x_turn(0)
+        rr_round(0)
         for t in range(NT):
-            rr(t)
+            if t + 1 < NT:
+                rr_round(t + 1)
+            rr_frac(t)
         trig_tile(0)
         x_quant(0)
         wprep(0, 0)
@@ -315,6 +341,7 @@ def tile_attentionalsplatting_pa_kernel(tc, tokens, tracks, w_k, k_gamma, out_0,
         x_turn(1)
         x_quant(1)
         x_turn(2)
+        x_turn(3)
         mm(0)
         mm(1)
         gamma_spread()
@@ -334,8 +361,9 @@ def tile_attentionalsplatting_pa_kernel(tc, tokens, tracks, w_k, k_gamma, out_0,
                 products(t, 1, (0,))
             if 0 <= t - 2 < NT:
                 row_max_scaled(t - 2)
+            if t + 2 < NT and t % 2 == 0:
+                x_quant_pair(t + 2)
             if t + 2 < NT:
-                x_quant(t + 2)
                 mm(t + 2)
             if 0 <= t - 2 < NT:
                 row_recip(t - 2)
@@ -346,7 +374,7 @@ def tile_attentionalsplatting_pa_kernel(tc, tokens, tracks, w_k, k_gamma, out_0,
                 cast_out(t - 2)
             if t < NT:
                 mean(t)
-            if t + 3 < NT:
-                x_turn(t + 3)
+            if t + 4 < NT:
+                x_turn(t + 4)
             if 0 <= t - 1 < NT:
                 gain(t - 1)

@@ -365,11 +365,11 @@ def tile_attentionalsplatting_pa_kernel(tc, tokens, tracks, w_k, k_gamma, out_0,
                 x_quant_pair(t + 2)
             if t + 2 < NT:
                 mm(t + 2)
-            if 0 <= t - 2 < NT:
-                row_recip(t - 2)
             if t < NT:
                 products(t, 1, (1,))
                 add(t)
+            if 0 <= t - 2 < NT:
+                row_recip(t - 2)
             if 0 <= t - 2 < NT:
                 cast_out(t - 2)
             if t < NT:

@@ -160,6 +160,26 @@ def tile_attentionalsplatting_pa_kernel(tc, tokens, tracks, w_k, k_gamma, out_0,
                     x_grouped[t + 1] = x_grouped[t]
                 turn(runs, None, x_grouped[t][:, (t % 2) * 2 * HALF : (t % 2 + 1) * 2 * HALF])
 
+        x_banks = {}
+
+        def x_transposes(t):
+            tp = tps.tile([P, 2, 2, P], F32, name="tp", tag="tp")
+            for g in (0, 1):
+                for u in (0, 1):
+                    nc.tensor.transpose(tp[:, g, u, :], x_words[t][:, 256 * g + u : 256 * (g + 1) : 2], ident[:])
+            x_banks[t] = tp
+
+        def x_copy_on_vector(t):
+            if t % 2 == 0:
+                x_grouped[t] = grp.tile([P, 4 * HALF], BF16, name="gr2", tag="gr2", bufs=2, align_bytes=64)
+                x_grouped[t + 1] = x_grouped[t]
+            nc.vector.tensor_copy(
+                out=x_grouped[t][:, (t % 2) * 2 * HALF : (t % 2 + 1) * 2 * HALF].bitcast(F32).rearrange(
+                    "p (g q u) -> p g q u", g=2, u=2
+                ),
+                in_=x_banks[t][:].rearrange("p g u q -> p g q u"),
+            )
+
         def x_quant(t):
             codes = const.tile([P, 2 * P], U32, name="xc%d" % t, align_bytes=64)
             scales = const.tile([P, 2 * P], U8, name="xs%d" % t, align_bytes=64)
@@ -347,6 +367,8 @@ def tile_attentionalsplatting_pa_kernel(tc, tokens, tracks, w_k, k_gamma, out_0,
         gamma_spread()
 
         for t in range(NT + 2):
+            if t + 4 < NT:
+                x_transposes(t + 4)
             if t < NT:
                 products(t, 0)
             if 0 <= t - 2 < NT:
@@ -375,6 +397,6 @@ def tile_attentionalsplatting_pa_kernel(tc, tokens, tracks, w_k, k_gamma, out_0,
             if t < NT:
                 mean(t)
             if t + 4 < NT:
-                x_turn(t + 4)
+                x_copy_on_vector(t + 4)
             if 0 <= t - 1 < NT:
                 gain(t - 1)

@@ -173,7 +173,7 @@ def tile_attentionalsplatting_pa_kernel(tc, tokens, tracks, w_k, k_gamma, out_0,
             if t % 2 == 0:
                 x_grouped[t] = grp.tile([P, 4 * HALF], BF16, name="gr2", tag="gr2", bufs=2, align_bytes=64)
                 x_grouped[t + 1] = x_grouped[t]
-            nc.vector.tensor_copy(
+            nc.scalar.copy(
                 out=x_grouped[t][:, (t % 2) * 2 * HALF : (t % 2 + 1) * 2 * HALF].bitcast(F32).rearrange(
                     "p (g q u) -> p g q u", g=2, u=2
                 ),

@@ -26,7 +26,7 @@ EPS = 1e-6
 TWO_PI = 2.0 * math.pi
 RATIO = 100.0 ** (-1.0 / 256.0)
 LAST = NT - 1
-SCALE_ON_G = (0, 1, 2, 3, 4, 5, 6)
+SCALE_ON_G = (0, 1, 2, 3)
 X_CHUNKS = ((0, 1), (1, 2), (2, 4), (4, 8))
 
 
@@ -279,8 +279,7 @@ def tile_attentionalsplatting_pa_kernel(tc, tokens, tracks, w_k, k_gamma, out_0,
         def add(t):
             d = st[t]
             d["rot"] = work.tile([P, C], F32, name="rot", tag="rot", bufs=2)
-            eng = nc.vector if t == LAST else nc.gpsimd
-            eng.tensor_tensor(
+            nc.gpsimd.tensor_tensor(
                 out=d["rot"][:], in0=d["t1"][:].rearrange("p s i -> p (s i)"),
                 in1=d["t2"][:].rearrange("p s i -> p (s i)"), op=ALU.add,
             )
@@ -293,7 +292,11 @@ def tile_attentionalsplatting_pa_kernel(tc, tokens, tracks, w_k, k_gamma, out_0,
             d["rstd"] = stat.tile([P, 1], F32, name="rstd", tag="rstd")
             nc.scalar.activation(out=junk[:], in_=d["rot"][:], func=ACT.Square, bias=d["negmu"][:, 0:1], scale=1.0, accum_out=ssq[:])
             nc.scalar.activation(out=ve[:], in_=ssq[:], func=ACT.Copy, scale=1.0 / C, bias=EPS)
-            nc.gpsimd.tensor_tensor(out=d["rstd"][:], in0=ve[:], in1=neghalf[:], op=ALU.pow)
+            d["ve"] = ve
+
+        def rstd_power(t):
+            d = st[t]
+            nc.gpsimd.tensor_tensor(out=d["rstd"][:], in0=d["ve"][:], in1=neghalf[:], op=ALU.pow)
 
         def gain(t):
             d = st[t]
@@ -309,8 +312,13 @@ def tile_attentionalsplatting_pa_kernel(tc, tokens, tracks, w_k, k_gamma, out_0,
             o0, y0, rstd = d["o0"], d["y0"], d["rstd"]
             if t in SCALE_ON_G:
                 nc.gpsimd.tensor_scalar(out=o0[:], in0=y0[:], scalar1=rstd[:, 0:1], scalar2=0.0, op0=ALU.mult, op1=ALU.add)
-            else:
+            elif t < LAST:
                 nc.scalar.activation(out=o0[:], in_=y0[:], func=ACT.Copy, scale=rstd[:, 0:1])
+            else:
+                nc.scalar.activation(out=o0[:, 0:HALF], in_=y0[:, 0:HALF], func=ACT.Copy, scale=rstd[:, 0:1])
+                nc.gpsimd.tensor_scalar(
+                    out=o0[:, HALF:C], in0=y0[:, HALF:C], scalar1=rstd[:, 0:1], scalar2=0.0, op0=ALU.mult, op1=ALU.add
+                )
             nc.sync.dma_start(out=o0_view[:, t, :], in_=o0[:])
 
         def row_max(t):
@@ -335,10 +343,11 @@ def tile_attentionalsplatting_pa_kernel(tc, tokens, tracks, w_k, k_gamma, out_0,
             r = d["ra"]
             q8 = work.tile([P, C], FP8, name="q8", tag="q8")
             o0 = d["o0"]
-            split = 384 if t == LAST else C
-            nc.scalar.activation(
-                out=q8[:, 0:split], in_=o0[:, 0:split], func=ACT.Identity, scale=r[:, 0:1], bias=zeros[:, 0:1], saturate=False
-            )
+            split = {LAST: 384, LAST - 1: 0}.get(t, C)
+            if split > 0:
+                nc.scalar.activation(
+                    out=q8[:, 0:split], in_=o0[:, 0:split], func=ACT.Identity, scale=r[:, 0:1], bias=zeros[:, 0:1], saturate=False
+                )
             if split < C:
                 nc.vector.tensor_scalar(
                     out=q8[:, split:C], in0=o0[:, split:C], scalar1=r[:, 0:1], scalar2=None, op0=ALU.mult, saturate=False
@@ -366,37 +375,51 @@ def tile_attentionalsplatting_pa_kernel(tc, tokens, tracks, w_k, k_gamma, out_0,
         mm(1)
         gamma_spread()
 
-        for t in range(NT + 2):
+        for t in range(NT):
             if t + 4 < NT:
                 x_transposes(t + 4)
-            if t < NT:
-                products(t, 0)
-            if 0 <= t - 2 < NT:
-                scale_out(t - 2)
+            products(t, 0)
             if t + 2 < NT:
                 trig_tile(t + 2)
-            if 0 <= t - 2 < NT:
+            if t >= 2:
                 row_max(t - 2)
-            if 0 <= t - 1 < NT:
+            if t >= 1:
                 variance(t - 1)
-            if t < NT:
-                products(t, 1, (0,))
-            if 0 <= t - 2 < NT:
+            if t >= 2 and t - 2 not in SCALE_ON_G:
+                scale_out(t - 2)
+            products(t, 1, (0,))
+            if t >= 2:
                 row_max_scaled(t - 2)
             if t + 2 < NT and t % 2 == 0:
                 x_quant_pair(t + 2)
             if t + 2 < NT:
                 mm(t + 2)
-            if t < NT:
-                products(t, 1, (1,))
-                add(t)
-            if 0 <= t - 2 < NT:
+            products(t, 1, (1,))
+            add(t)
+            if t >= 2:
                 row_recip(t - 2)
-            if 0 <= t - 2 < NT:
+            if t >= 1:
+                rstd_power(t - 1)
+            if t >= 2:
                 cast_out(t - 2)
-            if t < NT:
-                mean(t)
+            mean(t)
             if t + 4 < NT:
                 x_copy_on_vector(t + 4)
-            if 0 <= t - 1 < NT:
+            if t >= 1:
                 gain(t - 1)
+            if t >= 1 and t - 1 in SCALE_ON_G:
+                scale_out(t - 1)
+
+        row_max(LAST - 1)
+        variance(LAST)
+        rstd_power(LAST)
+        scale_out(LAST - 1)
+        gain(LAST)
+        row_max_scaled(LAST - 1)
+        row_max(LAST)
+        row_recip(LAST - 1)
+        row_max_scaled(LAST)
+        cast_out(LAST - 1)
+        row_recip(LAST)
+        scale_out(LAST)
+        cast_out(LAST)

@@ -364,11 +364,11 @@ def tile_attentionalsplatting_pa_kernel(tc, tokens, tracks, w_k, k_gamma, out_0,
         x_quant(0)
         wprep(0, 0)
         wprep(0, 1)
-        trig_tile(1)
         wprep(1, 0)
         wprep(1, 1)
         x_turn(1)
         x_quant(1)
+        trig_tile(1)
         x_turn(2)
         x_turn(3)
         mm(0)

@@ -390,12 +390,12 @@ def tile_attentionalsplatting_pa_kernel(tc, tokens, tracks, w_k, k_gamma, out_0,
             products(t, 1, (0,))
             if t >= 2:
                 row_max_scaled(t - 2)
+            products(t, 1, (1,))
+            add(t)
             if t + 2 < NT and t % 2 == 0:
                 x_quant_pair(t + 2)
             if t + 2 < NT:
                 mm(t + 2)
-            products(t, 1, (1,))
-            add(t)
             if t >= 2:
                 row_recip(t - 2)
             if t >= 1:

@@ -310,7 +310,7 @@ def tile_attentionalsplatting_pa_kernel(tc, tokens, tracks, w_k, k_gamma, out_0,
             d = st[t]
             d["o0"] = work.tile([P, C], F32, name="o0", tag="o0")
             o0, y0, rstd = d["o0"], d["y0"], d["rstd"]
-            if t in SCALE_ON_G:
+            if t in SCALE_ON_G or t == LAST - 1:
                 nc.gpsimd.tensor_scalar(out=o0[:], in0=y0[:], scalar1=rstd[:, 0:1], scalar2=0.0, op0=ALU.mult, op1=ALU.add)
             elif t < LAST:
                 nc.scalar.activation(out=o0[:], in_=y0[:], func=ACT.Copy, scale=rstd[:, 0:1])
@@ -343,7 +343,7 @@ def tile_attentionalsplatting_pa_kernel(tc, tokens, tracks, w_k, k_gamma, out_0,
             r = d["ra"]
             q8 = work.tile([P, C], FP8, name="q8", tag="q8")
             o0 = d["o0"]
-            split = {LAST: 384, LAST - 1: 0}.get(t, C)
+            split = 256 if t == LAST else C
             if split > 0:
                 nc.scalar.activation(
                     out=q8[:, 0:split], in_=o0[:, 0:split], func=ACT.Identity, scale=r[:, 0:1], bias=zeros[:, 0:1], saturate=False
@@ -375,7 +375,7 @@ def tile_attentionalsplatting_pa_kernel(tc, tokens, tracks, w_k, k_gamma, out_0,
         mm(1)
         gamma_spread()
 
-        for t in range(NT):
+        for t in range(NT - 1):
             if t + 4 < NT:
                 x_transposes(t + 4)
             products(t, 0)
@@ -410,16 +410,29 @@ def tile_attentionalsplatting_pa_kernel(tc, tokens, tracks, w_k, k_gamma, out_0,
             if t >= 1 and t - 1 in SCALE_ON_G:
                 scale_out(t - 1)
 
+        products(LAST, 0)
+        products(LAST, 1, (0,))
+        products(LAST, 1, (1,))
+        add(LAST)
+        row_max(LAST - 2)
+        variance(LAST - 1)
+        mean(LAST)
+        gain(LAST - 1)
+        rstd_power(LAST - 1)
+        row_max_scaled(LAST - 2)
+        scale_out(LAST - 2)
         row_max(LAST - 1)
+        row_recip(LAST - 2)
         variance(LAST)
-        rstd_power(LAST)
-        scale_out(LAST - 1)
         gain(LAST)
+        scale_out(LAST - 1)
+        rstd_power(LAST)
+        cast_out(LAST - 2)
         row_max_scaled(LAST - 1)
         row_max(LAST)
         row_recip(LAST - 1)
         row_max_scaled(LAST)
+        scale_out(LAST)
         cast_out(LAST - 1)
         row_recip(LAST)
-        scale_out(LAST)
         cast_out(LAST)

@@ -26,7 +26,7 @@ EPS = 1e-6
 TWO_PI = 2.0 * math.pi
 RATIO = 100.0 ** (-1.0 / 256.0)
 LAST = NT - 1
-SCALE_ON_G = (0, 1, 2, 3)
+SCALE_ON_G = (0, 1, 2)
 X_CHUNKS = ((0, 1), (1, 2), (2, 4), (4, 8))
 
 

import math
from contextlib import ExitStack

import concourse.mybir as mybir
from concourse.masks import make_identity

FLOPS = 2 * 1024 * 1024 * 1024

F32 = mybir.dt.float32
BF16 = mybir.dt.bfloat16
I32 = mybir.dt.int32
U32 = mybir.dt.uint32
U8 = mybir.dt.uint8
FP8X4 = mybir.dt.float8_e4m3fn_x4
FP8 = mybir.dt.float8_e4m3fn
ALU = mybir.AluOpType
ACT = mybir.ActivationFunctionType
AX = mybir.AxisListType

P = 128
NT = 8
K = 1024
C = 1024
HALF = 512
EPS = 1e-6
TWO_PI = 2.0 * math.pi
RATIO = 100.0 ** (-1.0 / 256.0)
LAST = NT - 1
SCALE_ON_G = (0, 1, 2)
X_CHUNKS = ((0, 1), (1, 2), (2, 4), (4, 8))


def tile_attentionalsplatting_pa_kernel(tc, tokens, tracks, w_k, k_gamma, out_0, out_1):
    nc = tc.nc
    x_view = tokens.flatten_outer_dims().rearrange("(p t) k -> p t k", t=NT)
    pos_view = tracks.flatten_outer_dims().rearrange("(p t) c -> p (t c)", t=NT)
    w_view = w_k.rearrange("(a b q h) k -> h a q b k", a=2, b=2, h=2)
    g_view = k_gamma.rearrange("(o c) -> o c", o=1)
    o0_view = out_0.flatten_outer_dims().rearrange("(p t) c -> p t c", t=NT)
    o1_view = out_1.flatten_outer_dims().rearrange("(p t) c -> p t c", t=NT)

    with ExitStack() as ctx:
        const = ctx.enter_context(tc.tile_pool(name="const", bufs=1))
        grp = ctx.enter_context(tc.tile_pool(name="grp", bufs=4))
        rrp = ctx.enter_context(tc.tile_pool(name="rrp", bufs=NT))
        trig = ctx.enter_context(tc.tile_pool(name="trig", bufs=4))
        work = ctx.enter_context(tc.tile_pool(name="work", bufs=3))
        stat = ctx.enter_context(tc.tile_pool(name="stat", bufs=4))
        tps = ctx.enter_context(tc.psum_pool(name="tps", bufs=3))
        gps = ctx.enter_context(tc.psum_pool(name="gps", bufs=1))
        accp = ctx.enter_context(tc.psum_pool(name="accp", bufs=2))
        ctx.enter_context(tc.manual_schedule())

        ident = const.tile([P, P], F32, name="ident")
        make_identity(nc, ident[:])
        ones_bf = const.tile([P, P], BF16, name="ones_bf")
        nc.gpsimd.memset(ones_bf[:], 1.0)
        neghalf = const.tile([P, 1], F32, name="neghalf")
        nc.gpsimd.memset(neghalf[:], -0.5)
        zeros = const.tile([P, 1], F32, name="zeros")
        nc.vector.memset(zeros[:], 0.0)
        one1 = const.tile([P, 1], F32, name="one1")
        nc.vector.memset(one1[:], 1.0)
        g_row = const.tile([P, C], BF16, name="g_row")
        nc.vector.memset(g_row[:], 0.0)
        warm = const.tile([P, 1], F32, name="warm")
        nc.scalar.activation(out=warm[:], in_=zeros[:], func=ACT.Sin)

        pos_bf = const.tile([P, 2 * NT], BF16, name="pos_bf")
        nc.sync.dma_start(out=pos_bf[:], in_=pos_view)
        x_words = {}

        def load_x(a, b):
            xr = const.tile([P, b - a, K], BF16, name="xr%d" % a)
            nc.sync.dma_start(out=xr[:], in_=x_view[:, a:b, :])
            for t in range(a, b):
                x_words[t] = xr[:, t - a, :].bitcast(F32)

        load_x(*X_CHUNKS[0])
        w_raw = {}
        for h in (0, 1):
            for a in (0, 1):
                wr = const.tile([P, 2, K], BF16, name="wr%d%d" % (h, a))
                nc.sync.dma_start(out=wr[:], in_=w_view[h, a])
                w_raw[(h, a)] = wr
        for a, b in X_CHUNKS[1:]:
            load_x(a, b)
        nc.scalar.dma_start(out=g_row[0:1, :], in_=g_view)

        theta = const.tile([P, 256], F32, name="theta")
        nc.vector.tensor_scalar(out=theta[:, 0:1], in0=one1[:], scalar1=1.0 / TWO_PI, scalar2=None, op0=ALU.mult)
        for s in (1, 4, 16, 64):
            for j in (1, 2, 3):
                nc.vector.tensor_scalar(
                    out=theta[:, j * s : (j + 1) * s], in0=theta[:, 0:s], scalar1=RATIO ** (j * s), scalar2=None, op0=ALU.mult
                )
        pos_f = const.tile([P, 2 * NT], F32, name="pos_f")
        nc.vector.tensor_copy(out=pos_f[:], in_=pos_bf[:])

        fracs = {}
        tables = {}

        turns = {}

        def rr_round(t):
            n_i = rrp.tile([P, HALF], I32, name="n_i", tag="n_i")
            for c in (0, 1):
                nc.vector.tensor_scalar(
                    out=n_i[:, 256 * c : 256 * (c + 1)], in0=theta[:], scalar1=pos_f[:, 2 * t + c : 2 * t + c + 1],
                    scalar2=None, op0=ALU.mult,
                )
            turns[t] = n_i

        def rr_frac(t):
            n_i = turns[t]
            f = rrp.tile([P, HALF], F32, name="f", tag="f")
            for c in (0, 1):
                nc.vector.scalar_tensor_tensor(
                    out=f[:, 256 * c : 256 * (c + 1)], in0=theta[:], scalar=pos_f[:, 2 * t + c : 2 * t + c + 1],
                    in1=n_i[:, 256 * c : 256 * (c + 1)], op0=ALU.mult, op1=ALU.subtract,
                )
            fracs[t] = f

        def trig_tile(t):
            f = fracs[t]
            af = work.tile([P, HALF], F32, name="af", tag="af", bufs=2)
            cos_sin = trig.tile([P, 2, HALF], F32, name="cos_sin", tag="cos_sin")
            nc.scalar.activation(out=af[:], in_=f[:], func=ACT.Abs)
            nc.scalar.activation(out=cos_sin[:, 0, :], in_=af[:], func=ACT.Sin, scale=-TWO_PI, bias=0.5 * math.pi)
            nc.scalar.activation(out=cos_sin[:, 1, :], in_=f[:], func=ACT.Sin, scale=TWO_PI)
            tables[t] = cos_sin

        def turn(word_runs, bank=None, grouped=None):
            if bank is None:
                tp = tps.tile([P, 2, 2, P], F32, name="tp", tag="tp")
            else:
                tp = accp.tile([P, 2, 2, P], F32, name="tp_" + bank, tag=bank)
            for g in (0, 1):
                for u in (0, 1):
                    nc.tensor.transpose(tp[:, g, u, :], word_runs[g][:, u : 2 * P : 2], ident[:])
            gr = grouped
            if gr is None:
                gr = grp.tile([P, 2 * HALF], BF16, name="gr", tag="gr", align_bytes=64)[:]
            nc.scalar.copy(
                out=gr.bitcast(F32).rearrange("p (g q u) -> p g q u", g=2, u=2), in_=tp[:].rearrange("p g u q -> p g q u")
            )
            return gr

        xc = {}
        xs = {}
        x_grouped = {}

        def x_turn(t):
            runs = [x_words[t][:, 256 * g : 256 * (g + 1)] for g in (0, 1)]
            if t < 2:
                x_grouped[t] = turn(runs)
            else:
                if t % 2 == 0:
                    x_grouped[t] = grp.tile([P, 4 * HALF], BF16, name="gr2", tag="gr2", bufs=2, align_bytes=64)
                    x_grouped[t + 1] = x_grouped[t]
                turn(runs, None, x_grouped[t][:, (t % 2) * 2 * HALF : (t % 2 + 1) * 2 * HALF])

        x_banks = {}

        def x_transposes(t):
            tp = tps.tile([P, 2, 2, P], F32, name="tp", tag="tp")
            for g in (0, 1):
                for u in (0, 1):
                    nc.tensor.transpose(tp[:, g, u, :], x_words[t][:, 256 * g + u : 256 * (g + 1) : 2], ident[:])
            x_banks[t] = tp

        def x_copy_on_vector(t):
            if t % 2 == 0:
                x_grouped[t] = grp.tile([P, 4 * HALF], BF16, name="gr2", tag="gr2", bufs=2, align_bytes=64)
                x_grouped[t + 1] = x_grouped[t]
            nc.scalar.copy(
                out=x_grouped[t][:, (t % 2) * 2 * HALF : (t % 2 + 1) * 2 * HALF].bitcast(F32).rearrange(
                    "p (g q u) -> p g q u", g=2, u=2
                ),
                in_=x_banks[t][:].rearrange("p g u q -> p g q u"),
            )

        def x_quant(t):
            codes = const.tile([P, 2 * P], U32, name="xc%d" % t, align_bytes=64)
            scales = const.tile([P, 2 * P], U8, name="xs%d" % t, align_bytes=64)
            nc.vector.quantize_mx(out=codes[:].bitcast(FP8X4), scales=scales[:], in_=x_grouped[t])
            xc[t] = codes[:]
            xs[t] = scales[:]

        def x_quant_pair(t):
            codes = const.tile([P, 4 * P], U32, name="xc%d" % t, align_bytes=64)
            scales = const.tile([P, 4 * P], U8, name="xs%d" % t, align_bytes=64)
            nc.vector.quantize_mx(out=codes[:].bitcast(FP8X4), scales=scales[:], in_=x_grouped[t][:])
            for e in (0, 1):
                xc[t + e] = codes[:, e * 2 * P : (e + 1) * 2 * P]
                xs[t + e] = scales[:, e * 2 * P : (e + 1) * 2 * P]

        wc = {}
        ws = {}
        for g in (0, 1):
            for h in (0, 1):
                wc[(g, h)] = const.tile([P, HALF], U32, name="wc%d%d" % (g, h), align_bytes=64)
                ws[(g, h)] = const.tile([P, HALF], U8, name="ws%d%d" % (g, h), align_bytes=64)

        w_grouped = {}

        def wprep(h, a):
            wr = w_raw[(h, a)]
            banks = ("acc0", "acc1") if a == 1 else (None, None)
            for g in (0, 1):
                if a == 0:
                    w_grouped[(g, h)] = const.tile([P, 4 * HALF], BF16, name="wg%d%d" % (g, h), align_bytes=64)
                turn(
                    [wr[:, b, :].bitcast(F32)[:, 256 * g : 256 * (g + 1)] for b in (0, 1)], banks[g],
                    w_grouped[(g, h)][:, a * 2 * HALF : (a + 1) * 2 * HALF],
                )
            if a == 1:
                for g in (0, 1):
                    nc.vector.quantize_mx(out=wc[(g, h)][:].bitcast(FP8X4), scales=ws[(g, h)][:], in_=w_grouped[(g, h)][:])

        gamma_ps = gps.tile([P, C], BF16, name="gamma_ps")

        def gamma_spread():
            for b in (0, 1):
                nc.tensor.matmul(
                    out=gamma_ps[:, b * HALF : (b + 1) * HALF], lhsT=ones_bf[:], rhs=g_row[:, b * HALF : (b + 1) * HALF],
                    start=True, stop=True,
                )

        st = {}

        def mm(t):
            acc = [accp.tile([P, HALF], F32, name="acc%d" % h, tag="acc%d" % h) for h in (0, 1)]
            for h in (0, 1):
                for g in (0, 1):
                    nc.tensor.matmul_mx(
                        out=acc[h][:],
                        lhsT=xc[t][:, g * P : (g + 1) * P].bitcast(FP8X4),
                        lhsT_scale=xs[t][:, g * P : (g + 1) * P],
                        rhs=wc[(g, h)][:].bitcast(FP8X4),
                        rhs_scale=ws[(g, h)][:],
                        start=(g == 0),
                        stop=(g == 1),
                    )
            st[t] = {"acc": acc}

        def products(t, h, parts=(0, 1)):
            d = st[t]
            if h == 0:
                d["t1"] = work.tile([P, 2, HALF], F32, name="t1", tag="t1", bufs=2)
                d["t2"] = work.tile([P, 2, HALF], F32, name="t2", tag="t2", bufs=2)
                d["sums"] = stat.tile([P, 3], F32, name="sums", tag="sums")
            k = d["acc"][h]
            cos_sin = tables[t]
            t1, t2, sums = d["t1"], d["t2"], d["sums"]
            stt = nc.vector.scalar_tensor_tensor
            if h == 0:
                stt(
                    out=t1[:], in0=k[:].unsqueeze(1).to_broadcast([P, 2, HALF]), scalar=1.0, in1=cos_sin[:],
                    op0=ALU.mult, op1=ALU.mult, accum_out=sums[:, 0:1],
                )
            if h == 1 and 0 in parts:
                stt(
                    out=t2[:, 0, :], in0=k[:], scalar=-1.0, in1=cos_sin[:, 1, :], op0=ALU.mult, op1=ALU.mult,
                    accum_out=sums[:, 1:2],
                )
            if h == 1 and 1 in parts:
                stt(
                    out=t2[:, 1, :], in0=k[:], scalar=1.0, in1=cos_sin[:, 0, :], op0=ALU.mult, op1=ALU.mult,
                    accum_out=sums[:, 2:3],
                )

        def mean(t):
            d = st[t]
            junk4 = stat.tile([P, 3], F32, name="junk4", tag="junk4")
            d["negmu"] = stat.tile([P, 1], F32, name="negmu", tag="negmu")
            nc.scalar.activation(out=junk4[:], in_=d["sums"][:], func=ACT.Identity, scale=-1.0 / C, accum_out=d["negmu"][:])

        def add(t):
            d = st[t]
            d["rot"] = work.tile([P, C], F32, name="rot", tag="rot", bufs=2)
            nc.gpsimd.tensor_tensor(
                out=d["rot"][:], in0=d["t1"][:].rearrange("p s i -> p (s i)"),
                in1=d["t2"][:].rearrange("p s i -> p (s i)"), op=ALU.add,
            )

        def variance(t):
            d = st[t]
            junk = work.tile([P, C], F32, name="junk", tag="junk", bufs=2)
            ssq = stat.tile([P, 1], F32, name="ssq", tag="ssq")
            ve = stat.tile([P, 1], F32, name="ve", tag="ve")
            d["rstd"] = stat.tile([P, 1], F32, name="rstd", tag="rstd")
            nc.scalar.activation(out=junk[:], in_=d["rot"][:], func=ACT.Square, bias=d["negmu"][:, 0:1], scale=1.0, accum_out=ssq[:])
            nc.scalar.activation(out=ve[:], in_=ssq[:], func=ACT.Copy, scale=1.0 / C, bias=EPS)
            d["ve"] = ve

        def rstd_power(t):
            d = st[t]
            nc.gpsimd.tensor_tensor(out=d["rstd"][:], in0=d["ve"][:], in1=neghalf[:], op=ALU.pow)

        def gain(t):
            d = st[t]
            d["y0"] = work.tile([P, C], F32, name="y0", tag="y0")
            nc.vector.scalar_tensor_tensor(
                out=d["y0"][:].rearrange("p (i s) -> p i s", s=2), in0=d["rot"][:].rearrange("p (s i) -> p i s", s=2),
                scalar=d["negmu"][:, 0:1], in1=gamma_ps[:].rearrange("p (i s) -> p i s", s=2), op0=ALU.add, op1=ALU.mult,
            )

        def scale_out(t):
            d = st[t]
            d["o0"] = work.tile([P, C], F32, name="o0", tag="o0")
            o0, y0, rstd = d["o0"], d["y0"], d["rstd"]
            if t in SCALE_ON_G or t == LAST - 1:
                nc.gpsimd.tensor_scalar(out=o0[:], in0=y0[:], scalar1=rstd[:, 0:1], scalar2=0.0, op0=ALU.mult, op1=ALU.add)
            elif t < LAST:
                nc.scalar.activation(out=o0[:], in_=y0[:], func=ACT.Copy, scale=rstd[:, 0:1])
            else:
                nc.scalar.activation(out=o0[:, 0:HALF], in_=y0[:, 0:HALF], func=ACT.Copy, scale=rstd[:, 0:1])
                nc.gpsimd.tensor_scalar(
                    out=o0[:, HALF:C], in0=y0[:, HALF:C], scalar1=rstd[:, 0:1], scalar2=0.0, op0=ALU.mult, op1=ALU.add
                )
            nc.sync.dma_start(out=o0_view[:, t, :], in_=o0[:])

        def row_max(t):
            d = st[t]
            d["amax_y"] = stat.tile([P, 1], F32, name="amax_y", tag="amax_y")
            nc.vector.tensor_reduce(out=d["amax_y"][:], in_=d["y0"][:], axis=AX.X, op=ALU.max, apply_absolute_value=True)

        def row_max_scaled(t):
            d = st[t]
            d["amax"] = stat.tile([P, 1], F32, name="amax", tag="amax")
            nc.vector.tensor_scalar(
                out=d["amax"][:], in0=d["amax_y"][:], scalar1=d["rstd"][:, 0:1], scalar2=1.0 / 448.0, op0=ALU.mult, op1=ALU.mult
            )

        def row_recip(t):
            d = st[t]
            d["ra"] = stat.tile([P, 1], F32, name="ra", tag="ra")
            nc.vector.reciprocal(out=d["ra"][:], in_=d["amax"][:])

        def cast_out(t):
            d = st[t]
            r = d["ra"]
            q8 = work.tile([P, C], FP8, name="q8", tag="q8")
            o0 = d["o0"]
            split = 256 if t == LAST else C
            if split > 0:
                nc.scalar.activation(
                    out=q8[:, 0:split], in_=o0[:, 0:split], func=ACT.Identity, scale=r[:, 0:1], bias=zeros[:, 0:1], saturate=False
                )
            if split < C:
                nc.vector.tensor_scalar(
                    out=q8[:, split:C], in0=o0[:, split:C], scalar1=r[:, 0:1], scalar2=None, op0=ALU.mult, saturate=False
                )
            nc.sync.dma_start(out=o1_view[:, t, :], in_=q8[:].bitcast(U8))

        x_turn(0)
        rr_round(0)
        for t in range(NT):
            if t + 1 < NT:
                rr_round(t + 1)
            rr_frac(t)
        trig_tile(0)
        x_quant(0)
        wprep(0, 0)
        wprep(0, 1)
        wprep(1, 0)
        wprep(1, 1)
        x_turn(1)
        x_quant(1)
        trig_tile(1)
        x_turn(2)
        x_turn(3)
        mm(0)
        mm(1)
        gamma_spread()

        for t in range(NT - 1):
            if t + 4 < NT:
                x_transposes(t + 4)
            products(t, 0)
            if t + 2 < NT:
                trig_tile(t + 2)
            if t >= 2:
                row_max(t - 2)
            if t >= 1:
                variance(t - 1)
            if t >= 2 and t - 2 not in SCALE_ON_G:
                scale_out(t - 2)
            products(t, 1, (0,))
            if t >= 2:
                row_max_scaled(t - 2)
            products(t, 1, (1,))
            add(t)
            if t + 2 < NT and t % 2 == 0:
                x_quant_pair(t + 2)
            if t + 2 < NT:
                mm(t + 2)
            if t >= 2:
                row_recip(t - 2)
            if t >= 1:
                rstd_power(t - 1)
            if t >= 2:
                cast_out(t - 2)
            mean(t)
            if t + 4 < NT:
                x_copy_on_vector(t + 4)
            if t >= 1:
                gain(t - 1)
            if t >= 1 and t - 1 in SCALE_ON_G:
                scale_out(t - 1)

        products(LAST, 0)
        products(LAST, 1, (0,))
        products(LAST, 1, (1,))
        add(LAST)
        row_max(LAST - 2)
        variance(LAST - 1)
        mean(LAST)
        gain(LAST - 1)
        rstd_power(LAST - 1)
        row_max_scaled(LAST - 2)
        scale_out(LAST - 2)
        row_max(LAST - 1)
        row_recip(LAST - 2)
        variance(LAST)
        gain(LAST)
        scale_out(LAST - 1)
        rstd_power(LAST)
        cast_out(LAST - 2)
        row_max_scaled(LAST - 1)
        row_max(LAST)
        row_recip(LAST - 1)
        row_max_scaled(LAST)
        scale_out(LAST)
        cast_out(LAST - 1)
        row_recip(LAST)
        cast_out(LAST)
